import numpy as np
import ml_dtypes


def mxq(x, axis, fmt="e4m3"):
    dtype, down = {"e4m3": (ml_dtypes.float8_e4m3fn, 7), "e5m2": (ml_dtypes.float8_e5m2, 14)}[fmt]
    v = np.moveaxis(np.asarray(x, np.float32).astype(ml_dtypes.bfloat16).astype(np.float64), axis, -1)
    blocks = v.reshape(v.shape[:-1] + (-1, 32))
    amax = np.abs(blocks).max(-1, keepdims=True)
    byte = np.maximum(np.where(amax > 0, np.frexp(amax)[1] - 1 + 127, 0) - down, 1)
    scale = np.exp2(byte - 127.0)
    codes = (blocks / scale).astype(np.float32).astype(dtype).astype(np.float64)
    return np.moveaxis((codes * scale).reshape(v.shape), -1, axis)


WIDE = False


def mx_kscale(k):
    if not WIDE:
        return np.ones(k)
    levels = np.array([10, -10, 5, -5, 0])
    if k % 512:
        return np.exp2(np.random.permutation(np.resize(levels, k // 32))).repeat(32)
    a = np.empty((k // 512, 16))
    for p in range(k // 512):
        a[p, :8] = np.random.permutation(np.resize(levels, 8))
        for g in range(8):
            far = levels[np.abs(levels - a[p, g]) >= 10]
            a[p, g + 8] = far[np.random.randint(len(far))]
    return np.exp2(a.ravel()).repeat(32)


BF16 = ml_dtypes.bfloat16


def bf(x):
    return np.asarray(x, np.float32).astype(BF16)


def f64(x):
    return np.asarray(x).astype(np.float64)


B, S, H, NH, LAT = 4, 2048, 512, 4, 512
HD = H // NH
HALF = H // 2
R = HALF // 2
ROPE_BASE = 10000.0


def rope_table():
    inv_freq = 1.0 / ROPE_BASE ** (np.arange(0, R, 2) / R)
    freqs = np.outer(np.arange(S), inv_freq)
    emb = np.concatenate([freqs, freqs], -1)
    return np.cos(emb), np.sin(emb)


def apply_rotary(x, cos, sin):
    h = x.shape[-1] // 2
    x1, x2 = x[..., :h], x[..., h:]
    return np.concatenate([x1 * cos - x2 * sin, x1 * sin + x2 * cos], -1)


def draw0():
    s, t = mx_kscale(H), mx_kscale(LAT)
    cos, sin = rope_table()
    return {"hidden_states": bf(np.random.standard_normal((B, S, H)) * s),
            "Wq_down": bf(np.random.standard_normal((LAT, H)) / np.sqrt(H) * t[:, None] / s),
            "bq_down": bf(np.random.standard_normal(LAT) * 0.2 * t),
            "Wq_up": bf(np.random.standard_normal((HALF, LAT)) * 1.2 / np.sqrt(LAT) / t),
            "bq_up": bf(np.random.standard_normal(HALF) * 0.2),
            "rope_cos": bf(cos),
            "rope_sin": bf(sin)}


def core(hidden_states, Wq_down, bq_down, Wq_up, bq_up, rope_cos, rope_sin):
    q_lat = (mxq(f64(hidden_states), 2, "e4m3") @ mxq(f64(Wq_down), 1, "e4m3").T) + f64(bq_down)
    q_half = (mxq(q_lat, 2, "e4m3") @ mxq(f64(Wq_up), 1, "e4m3").T) + f64(bq_up)
    q = np.concatenate([q_half, apply_rotary(q_half, f64(rope_cos), f64(rope_sin))], -1)
    return q.reshape(B, S, NH, HD).transpose(0, 2, 1, 3)


def e4m3fn_bytes(y):
    return np.clip(np.asarray(y, np.float64), -448.0, 448.0).astype(np.float32).astype(ml_dtypes.float8_e4m3fn).view(np.uint8)


def e4m3fn_values(b):
    return np.asarray(b, np.uint8).view(ml_dtypes.float8_e4m3fn).astype(np.float64)


def setup_inputs():
    d = draw0()
    x0 = np.asarray(d['hidden_states']).astype(np.float64)
    s = (np.max(np.abs(x0), axis=(0, 1), keepdims=True) / 448.0).astype(np.float32)
    out = {}
    for k, v in d.items():
        if k == 'hidden_states':
            out['hidden_states_bytes'] = e4m3fn_bytes(x0 / s.astype(np.float64))
            out['hidden_states_scale'] = s
        else:
            out[k] = v
    return out


def reference(hidden_states_bytes, hidden_states_scale, Wq_down, bq_down, Wq_up, bq_up, rope_cos, rope_sin):
    return core(e4m3fn_values(hidden_states_bytes) * hidden_states_scale.astype(np.float64), Wq_down, bq_down, Wq_up, bq_up, rope_cos, rope_sin)

from contextlib import ExitStack

import concourse.mybir as mybir
from concourse.masks import make_identity

F32 = mybir.dt.float32
BF16 = mybir.dt.bfloat16
U32 = mybir.dt.uint32
U8 = mybir.dt.uint8
FP8 = mybir.dt.float8_e4m3fn
FP8X4 = mybir.dt.float8_e4m3fn_x4
ADD = mybir.AluOpType.add
MULT = mybir.AluOpType.mult
COPY = mybir.ActivationFunctionType.Copy
IDENT = mybir.ActivationFunctionType.Identity

B, S, H, LAT, HALF = 4, 2048, 512, 512, 256
FLOPS = 2 * B * S * H * LAT + 2 * B * S * LAT * HALF

P = 128
T4 = 4
J = 4
GRP = P * J
PG = S // GRP
NG = B * PG


def tile_multiheadlatentattention_pa_t_kernel(
    tc, x_bytes, x_scale, wq_down, bq_down, wq_up, bq_up, rope_cos, rope_sin, out
):
    nc = tc.nc
    with ExitStack() as ctx:
        keep = ctx.enter_context(tc.tile_pool(name="keep", bufs=1))
        sb = ctx.enter_context(tc.tile_pool(name="sb", bufs=3))
        ps = ctx.enter_context(tc.psum_pool(name="ps", bufs=2))

        xb = {}

        def load_x(n):
            pg, b = divmod(n, B)
            t = sb.tile([P, J, H], U8, name="xbytes", bufs=6, align_bytes=64)
            nc.sync.dma_start(
                out=t[:],
                in_=x_bytes[b, pg * GRP : (pg + 1) * GRP, :].rearrange("(p j) k -> p j k", j=J),
            )
            xb[n] = t

        load_x(0)
        sc = keep.tile([P, T4], F32, name="sc")
        nc.sync.dma_start(out=sc[:], in_=x_scale.rearrange("a b (p t) -> p (a b t)", t=T4))
        wd = keep.tile([P, T4, H], BF16, name="wd", align_bytes=64)
        nc.sync.dma_start(out=wd[:], in_=wq_down.rearrange("(m t) k -> m t k", t=T4))
        load_x(1)
        bd = keep.tile([P, T4], BF16, name="bd")
        nc.sync.dma_start(out=bd[:], in_=bq_down.rearrange("(p t) -> p t", t=T4))
        wu = keep.tile([P, 2, LAT], BF16, name="wu", align_bytes=64)
        nc.sync.dma_start(out=wu[:], in_=wq_up.rearrange("(h m) k -> m h k", h=2))
        burow = keep.tile([P, P], BF16, name="burow")
        nc.gpsimd.memset(burow[:], 0.0)
        nc.sync.dma_start(out=burow[0:2, :], in_=bq_up.rearrange("(h c) -> h c", h=2))
        load_x(2)
        cosr = keep.tile([P, PG, J, P], BF16, name="cosr", align_bytes=64)
        sinr = keep.tile([P, PG, J, P], BF16, name="sinr", align_bytes=64)
        nc.sync.dma_start(out=cosr[:], in_=rope_cos.rearrange("(g p j) c -> p g j c", p=P, j=J))
        nc.sync.dma_start(out=sinr[:], in_=rope_sin.rearrange("(g p j) c -> p g j c", p=P, j=J))

        idf = keep.tile([P, P], F32, name="idf")
        make_identity(nc, idf[:])
        idb = keep.tile([P, P], BF16, name="idb")
        nc.vector.tensor_copy(out=idb[:], in_=idf[:])

        wdc = keep.tile([P, LAT], U32, name="wdc", align_bytes=64)
        wds = keep.tile([P, LAT], U8, name="wds", align_bytes=64)
        wuc = keep.tile([P, HALF], U32, name="wuc", align_bytes=64)
        wus = keep.tile([P, HALF], U8, name="wus", align_bytes=64)
        bu = keep.tile([P, 2], F32, name="bu")

        xbf, xt, xg, xc, xs, qg, qc, qs, m1, m2, qt, pa, pb, tab = ({} for i in range(14))

        def cast(n):
            t = sb.tile([P, J, H], BF16, name="xbf", align_bytes=64)
            nc.scalar.copy(out=t[:], in_=xb[n][:].bitcast(FP8))
            xbf[n] = t

        def turn(n, h):
            words = xbf[n][:].bitcast(F32)
            t = ps.tile([P, 2, 2 * P], F32, name="xt")
            for jj in range(2):
                for u in range(2):
                    nc.tensor.transpose(
                        t[:, u, jj * P : (jj + 1) * P], words[:, 2 * h + jj, u : H // 2 : 2], idf[:]
                    )
            xt[n, h] = t

        def scale(n, h):
            if h == 0:
                t = sb.tile([P, GRP, T4], BF16, name="xg", align_bytes=64)
                xg[n] = t
            nc.vector.tensor_tensor(
                out=xg[n][:, h * 2 * P : (h + 1) * 2 * P, :].rearrange("p r (u e) -> p r u e", e=2),
                in0=xt[n, h][:].bitcast(BF16).rearrange("p u (r e) -> p r u e", e=2),
                in1=sc[:].rearrange("p (u e) -> p u e", e=2).unsqueeze(1).to_broadcast([P, 2 * P, 2, 2]),
                op=MULT,
            )

        def quant_x(n):
            c = sb.tile([P, GRP], U32, name="xc", align_bytes=64)
            s = sb.tile([P, GRP], U8, name="xs", align_bytes=64)
            nc.vector.quantize_mx(
                out=c[:].bitcast(FP8X4), scales=s[:], in_=xg[n][:].rearrange("p r t -> p (r t)")
            )
            xc[n], xs[n] = c, s

        def down(n, j):
            t = ps.tile([P, T4, P], F32, name="m1")
            cols = slice(j * P, (j + 1) * P)
            for k in range(T4):
                ws = slice(k * P, (k + 1) * P)
                nc.tensor.matmul_mx(
                    out=t[:, k, :],
                    lhsT=wdc[:, ws].bitcast(FP8X4),
                    lhsT_scale=wds[:, ws],
                    rhs=xc[n][:, cols].bitcast(FP8X4),
                    rhs_scale=xs[n][:, cols],
                    start=True,
                    stop=True,
                )
            m1[n, j] = t

        def lat(n, j):
            if j == 0:
                t = sb.tile([P, GRP, T4], BF16, name="qg", align_bytes=64)
                qg[n] = t
            nc.vector.tensor_tensor(
                out=qg[n][:, j * P : (j + 1) * P, :],
                in0=m1[n, j][:].rearrange("p t r -> p r t"),
                in1=bd[:].unsqueeze(1).to_broadcast([P, P, T4]),
                op=ADD,
            )

        def quant_q(n):
            c = sb.tile([P, GRP], U32, name="qc", align_bytes=64)
            s = sb.tile([P, GRP], U8, name="qs", align_bytes=64)
            nc.vector.quantize_mx(
                out=c[:].bitcast(FP8X4), scales=s[:], in_=qg[n][:].rearrange("p r t -> p (r t)")
            )
            qc[n], qs[n] = c, s

        def up(n):
            for h in range(2):
                t = ps.tile([P, GRP], F32, name="m2")
                ws = slice(h * P, (h + 1) * P)
                nc.tensor.matmul_mx(
                    out=t[:],
                    lhsT=wuc[:, ws].bitcast(FP8X4),
                    lhsT_scale=wus[:, ws],
                    rhs=qc[n][:].bitcast(FP8X4),
                    rhs_scale=qs[n][:],
                    start=True,
                    stop=True,
                )
                m2[n, h] = t

        def half(n):
            t = sb.tile([P, 2, GRP], F32, name="qt")
            for h in range(2):
                nc.scalar.activation(
                    out=t[:, h, :], in_=m2[n, h][:], func=IDENT, bias=bu[:, h : h + 1]
                )
            qt[n] = t

        def products(n):
            pg = n // B
            a = sb.tile([P, 2, GRP], F32, name="pa")
            b = sb.tile([P, 2, GRP], F32, name="pb")
            for i in range(2):
                nc.gpsimd.tensor_tensor(
                    out=a[:, i, :], in0=qt[n][:, 0, :], in1=tab[pg][:, 1 + i, :], op=MULT
                )
                nc.gpsimd.tensor_tensor(
                    out=b[:, i, :], in0=qt[n][:, 1, :], in1=tab[pg][:, i, :], op=MULT
                )
            pa[n], pb[n] = a, b

        osb = {}

        def emit(n, j):
            if j == 0:
                t = sb.tile([P, 4, J, P], F32, name="osb", bufs=2)
                osb[n] = t
            o = ps.tile([P, 4, P], F32, name="ob")
            cols = slice(j * P, (j + 1) * P)
            for h in range(2):
                nc.tensor.transpose(o[:, h, :], qt[n][:, h, cols], idf[:])
            for i in range(2):
                nc.tensor.matmul(
                    o[:, 2 + i, :], lhsT=pa[n][:, i, cols], rhs=idf[:], start=True, stop=False, is_transpose=True
                )
                nc.tensor.matmul(
                    o[:, 2 + i, :], lhsT=pb[n][:, i, cols], rhs=idf[:], start=False, stop=True, is_transpose=True
                )
            nc.scalar.copy(out=osb[n][:, :, j, :], in_=o[:])
            if j == J - 1:
                pg, b = divmod(n, B)
                nc.sync.dma_start(
                    out=out[b, :, pg * GRP : (pg + 1) * GRP, :].rearrange("h (p j) d -> p h (j d)", j=J),
                    in_=osb[n][:].rearrange("p h j d -> p h (j d)"),
                )

        def table(pg):
            t = sb.tile([P, 3, GRP], BF16, name="tab", bufs=2)
            o = ps.tile([P, 2, J, P], BF16, name="ob")
            for i, src in enumerate((cosr, sinr)):
                for j in range(J):
                    nc.tensor.transpose(o[:, i, j, :], src[:, pg, j, :], idb[:])
            nc.scalar.copy(out=t[:, 1:3, :], in_=o[:].rearrange("p i j c -> p i (j c)"))
            nc.scalar.activation(
                out=t[:, 0, :], in_=o[:, 1, :, :].rearrange("p j c -> p (j c)"), func=COPY, scale=-1.0
            )
            tab[pg] = t

        def prep_down():
            g = keep.tile([P, LAT, T4], BF16, name="wdg", align_bytes=64)
            words = wd[:].bitcast(F32)
            for h in range(2):
                t = ps.tile([P, 2, 2 * P], F32, name="m1")
                for jj in range(2):
                    for u in range(2):
                        nc.tensor.transpose(
                            t[:, u, jj * P : (jj + 1) * P], words[:, 2 * h + jj, u : H // 2 : 2], idf[:]
                        )
                nc.scalar.copy(
                    out=g[:, h * 2 * P : (h + 1) * 2 * P, :].bitcast(F32), in_=t[:].rearrange("p u r -> p r u")
                )
            nc.vector.quantize_mx(
                out=wdc[:].bitcast(FP8X4), scales=wds[:], in_=g[:].rearrange("p r t -> p (r t)")
            )

        def prep_up():
            g = keep.tile([P, HALF, T4], BF16, name="wug", align_bytes=64)
            words = wu[:].bitcast(F32)
            t = ps.tile([P, 2, 2 * P], F32, name="m1")
            for h in range(2):
                for u in range(2):
                    nc.tensor.transpose(
                        t[:, u, h * P : (h + 1) * P], words[:, h, u : LAT // 2 : 2], idf[:]
                    )
            nc.scalar.copy(out=g[:].bitcast(F32), in_=t[:].rearrange("p u r -> p r u"))
            nc.vector.quantize_mx(
                out=wuc[:].bitcast(FP8X4), scales=wus[:], in_=g[:].rearrange("p r t -> p (r t)")
            )
            o = ps.tile([P, P], BF16, name="ob")
            nc.tensor.transpose(o[:], burow[:], idb[:])
            nc.scalar.copy(out=bu[:], in_=o[:, 0:2])

        def ok(n):
            return 0 <= n < NG

        with tc.manual_schedule():
            for s in range(-3, NG + 3):
                if ok(s + 6):
                    if s + 6 >= 3:
                        load_x(s + 6)
                if ok(s + 2):
                    turn(s + 2, 0)
                if ok(s + 3):
                    cast(s + 3)
                if s == -2:
                    prep_down()
                if s == -1:
                    prep_up()
                if ok(s):
                    down(s, 0)
                    down(s, 1)
                    lat(s, 0)
                    lat(s, 1)
                if ok(s + 2):
                    scale(s + 2, 0)
                if ok(s + 1):
                    quant_x(s + 1)
                if ok(s - 1):
                    up(s - 1)
                    half(s - 1)
                if ok(s - 3):
                    emit(s - 3, 0)
                    emit(s - 3, 1)
                if ok(s) and s % B == 0:
                    table(s // B)
                if ok(s + 2):
                    turn(s + 2, 1)
                if ok(s):
                    down(s, 2)
                    down(s, 3)
                    lat(s, 2)
                    lat(s, 3)
                if ok(s + 2):
                    scale(s + 2, 1)
                if ok(s):
                    quant_q(s)
                if ok(s - 2):
                    products(s - 2)
                if ok(s - 3):
                    emit(s - 3, 2)
                    emit(s - 3, 3)
